import numpy as np
import ml_dtypes


def mxq(x, axis, fmt="e4m3"):
    dtype, down = {"e4m3": (ml_dtypes.float8_e4m3fn, 7), "e5m2": (ml_dtypes.float8_e5m2, 14)}[fmt]
    v = np.moveaxis(np.asarray(x, np.float32).astype(ml_dtypes.bfloat16).astype(np.float64), axis, -1)
    blocks = v.reshape(v.shape[:-1] + (-1, 32))
    amax = np.abs(blocks).max(-1, keepdims=True)
    byte = np.maximum(np.where(amax > 0, np.frexp(amax)[1] - 1 + 127, 0) - down, 1)
    scale = np.exp2(byte - 127.0)
    codes = (blocks / scale).astype(np.float32).astype(dtype).astype(np.float64)
    return np.moveaxis((codes * scale).reshape(v.shape), -1, axis)


WIDE = False


def mx_kscale(k):
    if not WIDE:
        return np.ones(k)
    levels = np.array([10, -10, 5, -5, 0])
    a = np.random.permutation(np.resize(levels, k // 512 * 4)).reshape(k // 512, 4)
    idx = np.arange(k)
    return np.exp2(a[idx // 512, idx % 128 // 32])


BF16 = ml_dtypes.bfloat16


def bf(x):
    return np.asarray(x, np.float32).astype(BF16)


def f64(x):
    return np.asarray(x).astype(np.float64)


B, HEAD, NUM_EXPERTS, HEAD_DIM = 512, 4, 3, 512
EPS = 1e-5
VAR0 = 3e-4


def setup_inputs():
    s = mx_kscale(HEAD_DIM)
    p = (HEAD, NUM_EXPERTS, HEAD_DIM)

    def draw_x():
        return bf((np.random.standard_normal((B, HEAD, HEAD_DIM)) * s).reshape(B, HEAD * HEAD_DIM))

    return {"x1": draw_x(), "x2": draw_x(), "x3": draw_x(),
            "W": bf(np.random.standard_normal((HEAD, NUM_EXPERTS, HEAD_DIM, HEAD_DIM)) / np.sqrt(HEAD_DIM) / s),
            "b": bf(np.random.standard_normal(p) * 0.3),
            "gamma": bf(np.sqrt(VAR0) * (1.0 + 0.1 * np.random.standard_normal(p))),
            "beta": bf(np.random.standard_normal(p) * 0.3),
            "running_mean": bf(np.random.standard_normal(p) * 0.3),
            "running_var": bf(VAR0 * np.random.uniform(0.5, 1.5, p))}


def reference(x1, x2, x3, W, b, gamma, beta, running_mean, running_var):
    n = x1.shape[0]
    xs = np.stack([f64(x1).reshape(n, HEAD, HEAD_DIM),
                   f64(x2).reshape(n, HEAD, HEAD_DIM),
                   f64(x3).reshape(n, HEAD, HEAD_DIM)], axis=2)
    xq = mxq(xs, 3, "e4m3")
    wq = mxq(f64(W), 3, "e4m3")
    y = (xq.transpose(1, 2, 0, 3) @ wq.transpose(0, 1, 3, 2)).transpose(2, 0, 1, 3) + f64(b)
    y = y * (1.0 / (1.0 + np.exp(-1.702 * y)))
    y = (y - f64(running_mean)) * (1.0 / np.sqrt(f64(running_var) + EPS)) * f64(gamma) + f64(beta)
    return np.transpose(y, (0, 2, 1, 3)).reshape(n, NUM_EXPERTS * HEAD * HEAD_DIM)

@@ -1,0 +1,248 @@
+from contextlib import ExitStack
+
+import concourse.mybir as mybir
+from concourse.masks import make_identity
+
+F32 = mybir.dt.float32
+BF16 = mybir.dt.bfloat16
+U32 = mybir.dt.uint32
+U8 = mybir.dt.uint8
+FP8X4 = mybir.dt.float8_e4m3fn_x4
+ALU = mybir.AluOpType
+ACTF = mybir.ActivationFunctionType
+
+P = 128
+HEADS = 4
+EXPERTS = 3
+D = 512
+PAIRS = HEADS * EXPERTS
+EPS = 1e-5
+FLOPS = 2 * PAIRS * 512 * 512 * 512
+
+MANUAL = True
+AFFINE = "vector"
+TIN_EXIT = ("s", "s", "s", "v")
+TOUT_EXIT = ("v", "v", "v", "s")
+
+
+def tile_mom_kernel(tc, x1, x2, x3, W, b, gamma, beta, running_mean, running_var, out):
+    nc = tc.nc
+    xs = (x1, x2, x3)
+    with ExitStack() as ctx:
+        keep = ctx.enter_context(tc.tile_pool(name="keep", bufs=1))
+        grp = ctx.enter_context(tc.tile_pool(name="grp", bufs=2))
+        code = ctx.enter_context(tc.tile_pool(name="code", bufs=3))
+        zpool = ctx.enter_context(tc.tile_pool(name="zpool", bufs=3))
+        fpool = ctx.enter_context(tc.tile_pool(name="fpool", bufs=7))
+        psum = ctx.enter_context(tc.psum_pool(name="psum", bufs=1))
+        if MANUAL:
+            ctx.enter_context(tc.manual_schedule())
+
+        counter = [0]
+
+        def bank():
+            n = counter[0]
+            counter[0] = n + 1
+            return psum.tile([P, 512], F32, name="bk%d" % n, tag="bank%d" % (n % 8))
+
+        def copy_out(which, dst, src):
+            if which == "s":
+                nc.scalar.copy(out=dst, in_=src)
+            else:
+                nc.vector.tensor_copy(out=dst, in_=src)
+
+        raw = keep.tile([P, D], BF16, name="raw")
+        nc.vector.memset(raw[:].bitcast(mybir.dt.int32), 0)
+        one = keep.tile([P, 1], F32, name="one")
+        nc.vector.memset(one[:], 1.0)
+        ident = keep.tile([P, P], F32, name="ident")
+        make_identity(nc, ident[:])
+
+        x_sb = [keep.tile([P, 4 * HEADS * D], BF16, name="x_sb%d" % e) for e in range(EXPERTS)]
+        w_sb = [keep.tile([P, HEADS * 4 * D], BF16, name="w_sb%d" % e) for e in range(EXPERTS)]
+
+        def load_w(e, h0, h1):
+            nc.sync.dma_start(
+                out=w_sb[e][:].rearrange("p (h c) -> p h c", h=HEADS)[:, h0:h1, :],
+                in_=W[h0:h1, e].rearrange("h (p t) d -> p h (t d)", t=4),
+            )
+
+        def load_x(e, h0, h1):
+            nc.sync.dma_start(
+                out=x_sb[e][:].rearrange("p (j c) -> p j c", j=4)[:, :, D * h0:D * h1],
+                in_=xs[e].rearrange("(p j) c -> p j c", j=4)[:, :, D * h0:D * h1],
+            )
+
+        load_w(0, 0, 1)
+        load_x(0, 0, 1)
+        nc.scalar.dma_start(out=raw[0:12, :], in_=running_var.rearrange("h e f -> (h e) f"))
+        for i, prm in enumerate((b, gamma, beta, running_mean)):
+            nc.scalar.dma_start(out=raw[64 + 12 * i:76 + 12 * i, :], in_=prm.rearrange("h e f -> (h e) f"))
+        junk = keep.tile([P, 1], F32, name="junk")
+        nc.scalar.sqrt(out=junk[:], in_=one[:])
+        load_w(0, 1, 2)
+        load_x(0, 1, 2)
+        load_w(0, 2, 4)
+        load_x(0, 2, 4)
+        for e in (1, 2):
+            load_x(e, 0, 4)
+            load_w(e, 0, 4)
+
+        raw32 = keep.tile([P, 4, P], F32, name="raw32")
+        nc.gpsimd.tensor_scalar(
+            out=raw32[0:64], in0=raw[0:64, :].rearrange("r (p t) -> r t p", t=4),
+            scalar1=EPS, scalar2=1.0, op0=ALU.add, op1=ALU.mult,
+        )
+        nc.gpsimd.tensor_scalar(
+            out=raw32[64:128], in0=raw[64:128, :].rearrange("r (p t) -> r t p", t=4),
+            scalar1=1.0, scalar2=0.0, op0=ALU.mult, op1=ALU.add,
+        )
+        nc.scalar.sqrt(out=raw32[0:64], in_=raw32[0:64])
+        nc.scalar.activation(out=junk[:], in_=raw32[:, 0, 0:1], func=ACTF.Gelu_apprx_sigmoid)
+
+        NV = 4 * PAIRS
+        prm_t = keep.tile([P, P * 4], F32, name="prm_t")
+        std_t = prm_t[:, 0:NV]
+        bias_t = prm_t[:, 256:256 + NV]
+        gamma_t = prm_t[:, 256 + NV:256 + 2 * NV]
+        beta_t = prm_t[:, 256 + 2 * NV:256 + 3 * NV]
+        mean_t = prm_t[:, 256 + 3 * NV:256 + 4 * NV]
+        gain = keep.tile([P, NV], F32, name="gain")
+        shift = keep.tile([P, NV], F32, name="shift")
+
+        def params():
+            pbank = bank()
+            for t in range(4):
+                nc.tensor.transpose(pbank[:, P * t:P * t + P], raw32[:, t, :], ident[:])
+            nc.vector.tensor_copy(
+                out=prm_t[:].rearrange("p (r t) -> p r t", t=4)[:, 0:112, :],
+                in_=pbank[:].rearrange("p (t r) -> p r t", t=4)[:, 0:112, :],
+            )
+            nc.vector.reciprocal(out=gain[:], in_=std_t)
+            nc.vector.tensor_mul(out=gain[:], in0=gain[:], in1=gamma_t)
+            nc.vector.tensor_mul(out=shift[:], in0=mean_t, in1=gain[:])
+            nc.vector.tensor_sub(out=shift[:], in0=beta_t, in1=shift[:])
+
+        out_v = out.rearrange("(p j) c -> p j c", j=4)
+
+        codes = {}
+        zs = {}
+
+        def tin(k, exits):
+            e, h = divmod(k, HEADS)
+            srcs = (
+                w_sb[e][:].bitcast(F32)[:, 1024 * h:1024 * h + 1024],
+                x_sb[e][:].bitcast(F32),
+            )
+            gs = (
+                grp.tile([P, 4 * D], BF16, name="gw", align_bytes=64),
+                grp.tile([P, 4 * D], BF16, name="gx", align_bytes=64),
+            )
+            n = 0
+            for s in range(2):
+                g32 = gs[s][:].bitcast(F32).rearrange("q (c u) -> q c u", u=2)
+                for a in range(2):
+                    bk = bank()
+                    for r in (2 * a, 2 * a + 1):
+                        for u in range(2):
+                            if s == 0:
+                                c0 = 256 * r + P * u
+                            else:
+                                c0 = 1024 * r + 256 * h + P * u
+                            nc.tensor.transpose(
+                                bk[:, 256 * u + P * (r - 2 * a):256 * u + P * (r - 2 * a) + P],
+                                srcs[s][:, c0:c0 + P],
+                                ident[:],
+                            )
+                    copy_out(
+                        exits[n],
+                        g32[:, 256 * a:256 * a + 256, :],
+                        bk[:].rearrange("q (u c) -> q c u", u=2),
+                    )
+                    n += 1
+            return gs
+
+        def quant(k, gs):
+            cw = code.tile([P, D], U32, name="cw", align_bytes=64)
+            sw = code.tile([P, D], U8, name="sw", align_bytes=64)
+            cx = code.tile([P, D], U32, name="cx", align_bytes=64)
+            sx = code.tile([P, D], U8, name="sx", align_bytes=64)
+            nc.vector.quantize_mx(out=cw[:].bitcast(FP8X4), scales=sw[:], in_=gs[0][:])
+            nc.vector.quantize_mx(out=cx[:].bitcast(FP8X4), scales=sx[:], in_=gs[1][:])
+            codes[k] = (cw, sw, cx, sx)
+
+        def mx_gelu(k):
+            e, h = divmod(k, HEADS)
+            cw, sw, cx, sx = codes[k]
+            accs = []
+            for t in range(4):
+                acc = bank()
+                nc.tensor.matmul_mx(
+                    out=acc[:],
+                    lhsT=cw[:, P * t:P * t + P].bitcast(FP8X4),
+                    lhsT_scale=sw[:, P * t:P * t + P],
+                    rhs=cx[:].bitcast(FP8X4),
+                    rhs_scale=sx[:],
+                    start=True,
+                    stop=True,
+                )
+                accs.append(acc)
+            zt = []
+            for t in range(4):
+                col = 4 * (h * EXPERTS + e) + t
+                z = zpool.tile([P, 512], F32, name="z%d" % t)
+                nc.scalar.activation(
+                    out=z[:], in_=accs[t][:], func=ACTF.Gelu_apprx_sigmoid,
+                    bias=bias_t[:, col:col + 1], scale=1.0,
+                )
+                zt.append(z)
+            zs[k] = zt
+
+        def affine(k, t):
+            e, h = divmod(k, HEADS)
+            eng = nc.vector if AFFINE == "vector" else nc.gpsimd
+            col = 4 * (h * EXPERTS + e) + t
+            eng.tensor_scalar(
+                out=zs[k][t][:], in0=zs[k][t][:],
+                scalar1=gain[:, col:col + 1], scalar2=shift[:, col:col + 1],
+                op0=ALU.mult, op1=ALU.add,
+            )
+
+        def tout_and_affine(k, ka):
+            last = k == PAIRS - 1
+            if k >= 0:
+                fin = fpool.tile([P, 4, 512], F32, name="fin")
+                exits = ("v", "s", "v", "s") if k >= PAIRS - 2 else TOUT_EXIT
+                if last:
+                    bks = [bank() for j in range(4)]
+                    for t in range(4):
+                        for j in range(4):
+                            nc.tensor.transpose(bks[j][:, P * t:P * t + P], zs[k][t][:, P * j:P * j + P], ident[:])
+            for j in range(4):
+                if k >= 0:
+                    if last:
+                        bk = bks[j]
+                    else:
+                        bk = bank()
+                        for t in range(4):
+                            nc.tensor.transpose(bk[:, P * t:P * t + P], zs[k][t][:, P * j:P * j + P], ident[:])
+                    copy_out(
+                        exits[j],
+                        fin[:, j, :].rearrange("n (p t) -> n p t", t=4),
+                        bk[:].rearrange("n (t p) -> n p t", t=4),
+                    )
+                    if last:
+                        nc.sync.dma_start(out=out_v[:, j, 512 * k:512 * k + 512], in_=fin[:, j, :])
+                if 0 <= ka < PAIRS:
+                    affine(ka, j)
+            if k >= 0 and not last:
+                nc.sync.dma_start(out=out_v[:, :, 512 * k:512 * k + 512], in_=fin[:])
+
+        quant(0, tin(0, ("v", "v", "v", "v")))
+        params()
+        for k in range(0, PAIRS + 2):
+            tout_and_affine(k - 2, k - 1)
+            if k + 1 < PAIRS:
+                quant(k + 1, tin(k + 1, TIN_EXIT))
+            if k < PAIRS:
+                mx_gelu(k)

@@ -20,9 +20,8 @@ EPS = 1e-5
 FLOPS = 2 * PAIRS * 512 * 512 * 512
 
 MANUAL = True
-AFFINE = "vector"
-TIN_EXIT = ("s", "s", "s", "v")
-TOUT_EXIT = ("v", "v", "v", "s")
+TIN_EXIT = (("v", "s"), ("v", "s"))
+TOUT_EXIT = (("v", "v"), ("v", "s"))
 
 
 def tile_mom_kernel(tc, x1, x2, x3, W, b, gamma, beta, running_mean, running_var, out):
@@ -82,11 +81,14 @@ def tile_mom_kernel(tc, x1, x2, x3, W, b, gamma, beta, running_mean, running_var
         nc.scalar.sqrt(out=junk[:], in_=one[:])
         load_w(0, 1, 2)
         load_x(0, 1, 2)
-        load_w(0, 2, 4)
+        load_w(0, 2, 3)
         load_x(0, 2, 4)
+        load_w(0, 3, 4)
         for e in (1, 2):
             load_x(e, 0, 4)
-            load_w(e, 0, 4)
+            load_w(e, 0, 1)
+            load_w(e, 1, 2)
+            load_w(e, 2, 4)
 
         raw32 = keep.tile([P, 4, P], F32, name="raw32")
         nc.gpsimd.tensor_scalar(
@@ -128,54 +130,54 @@ def tile_mom_kernel(tc, x1, x2, x3, W, b, gamma, beta, running_mean, running_var
         codes = {}
         zs = {}
 
-        def tin(k, exits):
-            e, h = divmod(k, HEADS)
-            srcs = (
-                w_sb[e][:].bitcast(F32)[:, 1024 * h:1024 * h + 1024],
-                x_sb[e][:].bitcast(F32),
-            )
-            gs = (
-                grp.tile([P, 4 * D], BF16, name="gw", align_bytes=64),
-                grp.tile([P, 4 * D], BF16, name="gx", align_bytes=64),
-            )
-            n = 0
-            for s in range(2):
-                g32 = gs[s][:].bitcast(F32).rearrange("q (c u) -> q c u", u=2)
-                for a in range(2):
-                    bk = bank()
-                    for r in (2 * a, 2 * a + 1):
-                        for u in range(2):
-                            if s == 0:
-                                c0 = 256 * r + P * u
-                            else:
-                                c0 = 1024 * r + 256 * h + P * u
-                            nc.tensor.transpose(
-                                bk[:, 256 * u + P * (r - 2 * a):256 * u + P * (r - 2 * a) + P],
-                                srcs[s][:, c0:c0 + P],
-                                ident[:],
-                            )
-                    copy_out(
-                        exits[n],
-                        g32[:, 256 * a:256 * a + 256, :],
-                        bk[:].rearrange("q (u c) -> q c u", u=2),
-                    )
-                    n += 1
-            return gs
+        gtiles = {}
+        fins = {}
 
-        def quant(k, gs):
-            cw = code.tile([P, D], U32, name="cw", align_bytes=64)
-            sw = code.tile([P, D], U8, name="sw", align_bytes=64)
-            cx = code.tile([P, D], U32, name="cx", align_bytes=64)
-            sx = code.tile([P, D], U8, name="sx", align_bytes=64)
-            nc.vector.quantize_mx(out=cw[:].bitcast(FP8X4), scales=sw[:], in_=gs[0][:])
-            nc.vector.quantize_mx(out=cx[:].bitcast(FP8X4), scales=sx[:], in_=gs[1][:])
-            codes[k] = (cw, sw, cx, sx)
-
-        def mx_gelu(k):
+        def tin_half(k, s, exits):
             e, h = divmod(k, HEADS)
-            cw, sw, cx, sx = codes[k]
-            accs = []
-            for t in range(4):
+            if s == 0:
+                src = w_sb[e][:].bitcast(F32)[:, 1024 * h:1024 * h + 1024]
+                g = grp.tile([P, 4 * D], BF16, name="gw", align_bytes=64)
+            else:
+                src = x_sb[e][:].bitcast(F32)
+                g = grp.tile([P, 4 * D], BF16, name="gx", align_bytes=64)
+            g32 = g[:].bitcast(F32).rearrange("q (c u) -> q c u", u=2)
+            for a in range(2):
+                bk = bank()
+                for r in (2 * a, 2 * a + 1):
+                    for u in range(2):
+                        if s == 0:
+                            c0 = 256 * r + P * u
+                        else:
+                            c0 = 1024 * r + 256 * h + P * u
+                        nc.tensor.transpose(
+                            bk[:, 256 * u + P * (r - 2 * a):256 * u + P * (r - 2 * a) + P],
+                            src[:, c0:c0 + P],
+                            ident[:],
+                        )
+                copy_out(
+                    exits[a],
+                    g32[:, 256 * a:256 * a + 256, :],
+                    bk[:].rearrange("q (u c) -> q c u", u=2),
+                )
+            gtiles[(k, s)] = g
+
+        def quant_half(k, s):
+            if s == 0:
+                c = code.tile([P, D], U32, name="cw", align_bytes=64)
+                sc = code.tile([P, D], U8, name="sw", align_bytes=64)
+            else:
+                c = code.tile([P, D], U32, name="cx", align_bytes=64)
+                sc = code.tile([P, D], U8, name="sx", align_bytes=64)
+            nc.vector.quantize_mx(out=c[:].bitcast(FP8X4), scales=sc[:], in_=gtiles[(k, s)][:])
+            codes[(k, s)] = (c, sc)
+
+        def mx_gelu(k, ts):
+            e, h = divmod(k, HEADS)
+            cw, sw = codes[(k, 0)]
+            cx, sx = codes[(k, 1)]
+            accs = {}
+            for t in ts:
                 acc = bank()
                 nc.tensor.matmul_mx(
                     out=acc[:],
@@ -186,63 +188,63 @@ def tile_mom_kernel(tc, x1, x2, x3, W, b, gamma, beta, running_mean, running_var
                     start=True,
                     stop=True,
                 )
-                accs.append(acc)
-            zt = []
-            for t in range(4):
+                accs[t] = acc
+            eng = nc.vector if k == PAIRS - 1 else nc.gpsimd
+            for t in ts:
                 col = 4 * (h * EXPERTS + e) + t
                 z = zpool.tile([P, 512], F32, name="z%d" % t)
                 nc.scalar.activation(
                     out=z[:], in_=accs[t][:], func=ACTF.Gelu_apprx_sigmoid,
                     bias=bias_t[:, col:col + 1], scale=1.0,
                 )
-                zt.append(z)
-            zs[k] = zt
+                eng.tensor_scalar(
+                    out=z[:], in0=z[:],
+                    scalar1=gain[:, col:col + 1], scalar2=shift[:, col:col + 1],
+                    op0=ALU.mult, op1=ALU.add,
+                )
+                zs[(k, t)] = z
 
-        def affine(k, t):
-            e, h = divmod(k, HEADS)
-            eng = nc.vector if AFFINE == "vector" else nc.gpsimd
-            col = 4 * (h * EXPERTS + e) + t
-            eng.tensor_scalar(
-                out=zs[k][t][:], in0=zs[k][t][:],
-                scalar1=gain[:, col:col + 1], scalar2=shift[:, col:col + 1],
-                op0=ALU.mult, op1=ALU.add,
+        def fin_copy(k, j, bk, which):
+            copy_out(
+                which,
+                fins[k][:, j, :].rearrange("n (p t) -> n p t", t=4),
+                bk[:].rearrange("n (t p) -> n p t", t=4),
             )
 
-        def tout_and_affine(k, ka):
-            last = k == PAIRS - 1
-            if k >= 0:
-                fin = fpool.tile([P, 4, 512], F32, name="fin")
-                exits = ("v", "s", "v", "s") if k >= PAIRS - 2 else TOUT_EXIT
-                if last:
-                    bks = [bank() for j in range(4)]
-                    for t in range(4):
-                        for j in range(4):
-                            nc.tensor.transpose(bks[j][:, P * t:P * t + P], zs[k][t][:, P * j:P * j + P], ident[:])
-            for j in range(4):
-                if k >= 0:
-                    if last:
-                        bk = bks[j]
-                    else:
-                        bk = bank()
-                        for t in range(4):
-                            nc.tensor.transpose(bk[:, P * t:P * t + P], zs[k][t][:, P * j:P * j + P], ident[:])
-                    copy_out(
-                        exits[j],
-                        fin[:, j, :].rearrange("n (p t) -> n p t", t=4),
-                        bk[:].rearrange("n (t p) -> n p t", t=4),
-                    )
-                    if last:
-                        nc.sync.dma_start(out=out_v[:, j, 512 * k:512 * k + 512], in_=fin[:, j, :])
-                if 0 <= ka < PAIRS:
-                    affine(ka, j)
-            if k >= 0 and not last:
-                nc.sync.dma_start(out=out_v[:, :, 512 * k:512 * k + 512], in_=fin[:])
+        def tout_half(k, hf, exits):
+            if hf == 0:
+                fins[k] = fpool.tile([P, 4, 512], F32, name="fin")
+            for j in (2 * hf, 2 * hf + 1):
+                bk = bank()
+                for t in range(4):
+                    nc.tensor.transpose(bk[:, P * t:P * t + P], zs[(k, t)][:, P * j:P * j + P], ident[:])
+                fin_copy(k, j, bk, exits[j - 2 * hf])
+            nc.sync.dma_start(
+                out=out_v[:, 2 * hf:2 * hf + 2, 512 * k:512 * k + 512],
+                in_=fins[k][:, 2 * hf:2 * hf + 2, :],
+            )
 
-        quant(0, tin(0, ("v", "v", "v", "v")))
+        def tout_last(k):
+            fins[k] = fpool.tile([P, 4, 512], F32, name="fin")
+            bks = [bank() for j in range(4)]
+            for t in range(4):
+                for j in range(4):
+                    nc.tensor.transpose(bks[j][:, P * t:P * t + P], zs[(k, t)][:, P * j:P * j + P], ident[:])
+            for j in range(4):
+                fin_copy(k, j, bks[j], ("v", "s")[j % 2])
+                nc.sync.dma_start(out=out_v[:, j, 512 * k:512 * k + 512], in_=fins[k][:, j, :])
+
+        for s in range(2):
+            tin_half(0, s, ("v", "v"))
+            quant_half(0, s)
         params()
-        for k in range(0, PAIRS + 2):
-            tout_and_affine(k - 2, k - 1)
-            if k + 1 < PAIRS:
-                quant(k + 1, tin(k + 1, TIN_EXIT))
-            if k < PAIRS:
-                mx_gelu(k)
+        for k in range(0, PAIRS + 1):
+            for hf in range(2):
+                if 0 <= k - 2:
+                    tout_half(k - 2, hf, ("v", "s") if k - 2 == PAIRS - 2 else TOUT_EXIT[hf])
+                if k + 1 < PAIRS:
+                    tin_half(k + 1, hf, TIN_EXIT[hf])
+                    quant_half(k + 1, hf)
+                if k < PAIRS:
+                    mx_gelu(k, (2 * hf, 2 * hf + 1))
+        tout_last(PAIRS - 1)

@@ -20,8 +20,8 @@ EPS = 1e-5
 FLOPS = 2 * PAIRS * 512 * 512 * 512
 
 MANUAL = True
-TIN_EXIT = (("v", "s"), ("v", "s"))
-TOUT_EXIT = (("v", "v"), ("v", "s"))
+TIN_EXIT = (("s", "s"), ("s", "s"))
+TOUT_EXIT = (("v", "v"), ("v", "v"))
 
 
 def tile_mom_kernel(tc, x1, x2, x3, W, b, gamma, beta, running_mean, running_var, out):
@@ -189,7 +189,6 @@ def tile_mom_kernel(tc, x1, x2, x3, W, b, gamma, beta, running_mean, running_var
                     stop=True,
                 )
                 accs[t] = acc
-            eng = nc.vector if k == PAIRS - 1 else nc.gpsimd
             for t in ts:
                 col = 4 * (h * EXPERTS + e) + t
                 z = zpool.tile([P, 512], F32, name="z%d" % t)
@@ -197,12 +196,17 @@ def tile_mom_kernel(tc, x1, x2, x3, W, b, gamma, beta, running_mean, running_var
                     out=z[:], in_=accs[t][:], func=ACTF.Gelu_apprx_sigmoid,
                     bias=bias_t[:, col:col + 1], scale=1.0,
                 )
-                eng.tensor_scalar(
-                    out=z[:], in0=z[:],
-                    scalar1=gain[:, col:col + 1], scalar2=shift[:, col:col + 1],
-                    op0=ALU.mult, op1=ALU.add,
-                )
                 zs[(k, t)] = z
+
+        def affine(k, t):
+            e, h = divmod(k, HEADS)
+            col = 4 * (h * EXPERTS + e) + t
+            z = zs[(k, t)]
+            nc.vector.tensor_scalar(
+                out=z[:], in0=z[:],
+                scalar1=gain[:, col:col + 1], scalar2=shift[:, col:col + 1],
+                op0=ALU.mult, op1=ALU.add,
+            )
 
         def fin_copy(k, j, bk, which):
             copy_out(
@@ -238,13 +242,22 @@ def tile_mom_kernel(tc, x1, x2, x3, W, b, gamma, beta, running_mean, running_var
             tin_half(0, s, ("v", "v"))
             quant_half(0, s)
         params()
+        pend_q = []
+        pend_a = []
         for k in range(0, PAIRS + 1):
             for hf in range(2):
+                for kk, s in pend_q:
+                    quant_half(kk, s)
+                pend_q = []
                 if 0 <= k - 2:
                     tout_half(k - 2, hf, ("v", "s") if k - 2 == PAIRS - 2 else TOUT_EXIT[hf])
+                for kk, t in pend_a:
+                    affine(kk, t)
+                pend_a = []
                 if k + 1 < PAIRS:
                     tin_half(k + 1, hf, TIN_EXIT[hf])
-                    quant_half(k + 1, hf)
+                    pend_q = [(k + 1, hf)]
                 if k < PAIRS:
                     mx_gelu(k, (2 * hf, 2 * hf + 1))
+                    pend_a = [(k, 2 * hf), (k, 2 * hf + 1)]
         tout_last(PAIRS - 1)

@@ -50,14 +50,28 @@ def tile_mom_kernel(tc, x1, x2, x3, W, b, gamma, beta, running_mean, running_var
             else:
                 nc.vector.tensor_copy(out=dst, in_=src)
 
-        raw = keep.tile([P, D], BF16, name="raw")
-        nc.vector.memset(raw[:].bitcast(mybir.dt.int32), 0)
+        raw = keep.tile([P, 3 * P], BF16, name="raw")
+        vraw = keep.tile([P, 3 * P], BF16, name="vraw")
+
+        def load_rows(dst, r0, prm):
+            nc.sync.dma_start(
+                out=dst[r0:r0 + 16, :],
+                in_=prm.rearrange("h e f -> (h e f)").rearrange("(q c) -> q c", q=16),
+            )
+
+        load_rows(vraw, 0, running_var)
         one = keep.tile([P, 1], F32, name="one")
         nc.vector.memset(one[:], 1.0)
+        raw32 = keep.tile([P, 3 * P], F32, name="raw32")
+        nc.vector.memset(raw32[:], 0.0)
+        nc.vector.tensor_scalar(
+            out=raw32[0:16, :], in0=vraw[0:16, :],
+            scalar1=EPS, scalar2=1.0, op0=ALU.add, op1=ALU.mult,
+        )
         ident = keep.tile([P, P], F32, name="ident")
         make_identity(nc, ident[:])
 
-        x_sb = [keep.tile([P, 4 * HEADS * D], BF16, name="x_sb%d" % e) for e in range(EXPERTS)]
+        x_sb = {}
         w_sb = [keep.tile([P, HEADS * 4 * D], BF16, name="w_sb%d" % e) for e in range(EXPERTS)]
 
         def load_w(e, h0, h1):
@@ -67,16 +81,18 @@ def tile_mom_kernel(tc, x1, x2, x3, W, b, gamma, beta, running_mean, running_var
             )
 
         def load_x(e, h0, h1):
+            xt = keep.tile([P, 4 * D * (h1 - h0)], BF16, name="x_sb%d_%d" % (e, h0))
             nc.sync.dma_start(
-                out=x_sb[e][:].rearrange("p (j c) -> p j c", j=4)[:, :, D * h0:D * h1],
+                out=xt[:].rearrange("p (j c) -> p j c", j=4),
                 in_=xs[e].rearrange("(p j) c -> p j c", j=4)[:, :, D * h0:D * h1],
             )
+            for h in range(h0, h1):
+                x_sb[(e, h)] = (xt, h - h0, h1 - h0)
 
         load_w(0, 0, 1)
         load_x(0, 0, 1)
-        nc.scalar.dma_start(out=raw[0:12, :], in_=running_var.rearrange("h e f -> (h e) f"))
         for i, prm in enumerate((b, gamma, beta, running_mean)):
-            nc.scalar.dma_start(out=raw[64 + 12 * i:76 + 12 * i, :], in_=prm.rearrange("h e f -> (h e) f"))
+            load_rows(raw, 64 + 16 * i, prm)
         junk = keep.tile([P, 1], F32, name="junk")
         nc.scalar.sqrt(out=junk[:], in_=one[:])
         load_w(0, 1, 2)
@@ -90,35 +106,35 @@ def tile_mom_kernel(tc, x1, x2, x3, W, b, gamma, beta, running_mean, running_var
             load_w(e, 1, 2)
             load_w(e, 2, 4)
 
-        raw32 = keep.tile([P, 4, P], F32, name="raw32")
+        nc.scalar.sqrt(out=raw32[0:16, :], in_=raw32[0:16, :])
+        nc.scalar.activation(out=junk[:], in_=one[:], func=ACTF.Gelu_apprx_sigmoid)
         nc.gpsimd.tensor_scalar(
-            out=raw32[0:64], in0=raw[0:64, :].rearrange("r (p t) -> r t p", t=4),
-            scalar1=EPS, scalar2=1.0, op0=ALU.add, op1=ALU.mult,
-        )
-        nc.gpsimd.tensor_scalar(
-            out=raw32[64:128], in0=raw[64:128, :].rearrange("r (p t) -> r t p", t=4),
+            out=raw32[64:128, :], in0=raw[64:128, :],
             scalar1=1.0, scalar2=0.0, op0=ALU.mult, op1=ALU.add,
         )
-        nc.scalar.sqrt(out=raw32[0:64], in_=raw32[0:64])
-        nc.scalar.activation(out=junk[:], in_=raw32[:, 0, 0:1], func=ACTF.Gelu_apprx_sigmoid)
 
         NV = 4 * PAIRS
-        prm_t = keep.tile([P, P * 4], F32, name="prm_t")
+        prm_t = keep.tile([P, P * 3], F32, name="prm_t")
         std_t = prm_t[:, 0:NV]
-        bias_t = prm_t[:, 256:256 + NV]
-        gamma_t = prm_t[:, 256 + NV:256 + 2 * NV]
-        beta_t = prm_t[:, 256 + 2 * NV:256 + 3 * NV]
-        mean_t = prm_t[:, 256 + 3 * NV:256 + 4 * NV]
+        bias_t = prm_t[:, 192:192 + NV]
+        gamma_t = prm_t[:, 192 + NV:192 + 2 * NV]
+        beta_t = prm_t[:, 192 + 2 * NV:192 + 3 * NV]
+        mean_t = prm_t[:, 192 + 3 * NV:192 + 4 * NV]
         gain = keep.tile([P, NV], F32, name="gain")
         shift = keep.tile([P, NV], F32, name="shift")
 
+        pbanks = []
+
+        def params_turn():
+            pbanks.append(bank())
+            for v in range(3):
+                nc.tensor.transpose(pbanks[0][:, P * v:P * v + P], raw32[:, P * v:P * v + P], ident[:])
+
         def params():
-            pbank = bank()
-            for t in range(4):
-                nc.tensor.transpose(pbank[:, P * t:P * t + P], raw32[:, t, :], ident[:])
+            pbank = pbanks[0]
             nc.vector.tensor_copy(
-                out=prm_t[:].rearrange("p (r t) -> p r t", t=4)[:, 0:112, :],
-                in_=pbank[:].rearrange("p (t r) -> p r t", t=4)[:, 0:112, :],
+                out=prm_t[:].rearrange("p (r v) -> p r v", v=3),
+                in_=pbank[:, 0:3 * P].rearrange("p (v r) -> p r v", v=3),
             )
             nc.vector.reciprocal(out=gain[:], in_=std_t)
             nc.vector.tensor_mul(out=gain[:], in0=gain[:], in1=gamma_t)
@@ -139,9 +155,10 @@ def tile_mom_kernel(tc, x1, x2, x3, W, b, gamma, beta, running_mean, running_var
                 src = w_sb[e][:].bitcast(F32)[:, 1024 * h:1024 * h + 1024]
                 g = grp.tile([P, 4 * D], BF16, name="gw", align_bytes=64)
             else:
-                src = x_sb[e][:].bitcast(F32)
+                xt, hx, nx = x_sb[(e, h)]
+                src = xt[:].bitcast(F32)
                 g = grp.tile([P, 4 * D], BF16, name="gx", align_bytes=64)
-            g32 = g[:].bitcast(F32).rearrange("q (c u) -> q c u", u=2)
+            g32 = g[:].bitcast(F32)
             for a in range(2):
                 bk = bank()
                 for r in (2 * a, 2 * a + 1):
@@ -149,17 +166,24 @@ def tile_mom_kernel(tc, x1, x2, x3, W, b, gamma, beta, running_mean, running_var
                         if s == 0:
                             c0 = 256 * r + P * u
                         else:
-                            c0 = 1024 * r + 256 * h + P * u
+                            c0 = 256 * nx * r + 256 * hx + P * u
                         nc.tensor.transpose(
                             bk[:, 256 * u + P * (r - 2 * a):256 * u + P * (r - 2 * a) + P],
                             src[:, c0:c0 + P],
                             ident[:],
                         )
-                copy_out(
-                    exits[a],
-                    g32[:, 256 * a:256 * a + 256, :],
-                    bk[:].rearrange("q (u c) -> q c u", u=2),
-                )
+                if s == 0:
+                    copy_out(
+                        exits[a],
+                        g32.rearrange("q (c r u) -> q c r u", r=4, u=2)[:, :, 2 * a:2 * a + 2, :],
+                        bk[:].rearrange("q (u r c) -> q c r u", u=2, r=2),
+                    )
+                else:
+                    copy_out(
+                        exits[a],
+                        g32.rearrange("q (c u) -> q c u", u=2)[:, 256 * a:256 * a + 256, :],
+                        bk[:].rearrange("q (u c) -> q c u", u=2),
+                    )
             gtiles[(k, s)] = g
 
         def quant_half(k, s):
@@ -209,11 +233,7 @@ def tile_mom_kernel(tc, x1, x2, x3, W, b, gamma, beta, running_mean, running_var
             )
 
         def fin_copy(k, j, bk, which):
-            copy_out(
-                which,
-                fins[k][:, j, :].rearrange("n (p t) -> n p t", t=4),
-                bk[:].rearrange("n (t p) -> n p t", t=4),
-            )
+            copy_out(which, fins[k][:, j, :], bk[:])
 
         def tout_half(k, hf, exits):
             if hf == 0:
@@ -238,9 +258,11 @@ def tile_mom_kernel(tc, x1, x2, x3, W, b, gamma, beta, running_mean, running_var
                 fin_copy(k, j, bks[j], ("v", "s")[j % 2])
                 nc.sync.dma_start(out=out_v[:, j, 512 * k:512 * k + 512], in_=fins[k][:, j, :])
 
-        for s in range(2):
-            tin_half(0, s, ("v", "v"))
-            quant_half(0, s)
+        tin_half(0, 0, ("v", "v"))
+        quant_half(0, 0)
+        tin_half(0, 1, ("s", "v"))
+        params_turn()
+        quant_half(0, 1)
         params()
         pend_q = []
         pend_a = []

@@ -89,10 +89,23 @@ def tile_mom_kernel(tc, x1, x2, x3, W, b, gamma, beta, running_mean, running_var
             for h in range(h0, h1):
                 x_sb[(e, h)] = (xt, h - h0, h1 - h0)
 
-        load_w(0, 0, 1)
-        load_x(0, 0, 1)
+        for a in range(2):
+            nc.sync.dma_start(
+                out=w_sb[0][:, 2 * D * a:2 * D * a + 2 * D],
+                in_=W[0, 0].rearrange("(p t) d -> p (t d)", t=4)[:, 2 * D * a:2 * D * a + 2 * D],
+            )
+        x00 = keep.tile([P, 4 * D], BF16, name="x_sb0_0")
+        x_sb[(0, 0)] = (x00, 0, 1)
+        nc.sync.dma_start(
+            out=x00[:, 0:2 * D].rearrange("p (j c) -> p j c", j=2),
+            in_=xs[0].rearrange("(p j) c -> p j c", j=4)[:, 0:2, 0:D],
+        )
         for i, prm in enumerate((b, gamma, beta, running_mean)):
             load_rows(raw, 64 + 16 * i, prm)
+        nc.sync.dma_start(
+            out=x00[:, 2 * D:4 * D].rearrange("p (j c) -> p j c", j=2),
+            in_=xs[0].rearrange("(p j) c -> p j c", j=4)[:, 2:4, 0:D],
+        )
         junk = keep.tile([P, 1], F32, name="junk")
         nc.scalar.sqrt(out=junk[:], in_=one[:])
         load_w(0, 1, 2)

from contextlib import ExitStack

import concourse.mybir as mybir
from concourse.masks import make_identity

F32 = mybir.dt.float32
BF16 = mybir.dt.bfloat16
U32 = mybir.dt.uint32
U8 = mybir.dt.uint8
FP8X4 = mybir.dt.float8_e4m3fn_x4
ALU = mybir.AluOpType
ACTF = mybir.ActivationFunctionType

P = 128
HEADS = 4
EXPERTS = 3
D = 512
PAIRS = HEADS * EXPERTS
EPS = 1e-5
FLOPS = 2 * PAIRS * 512 * 512 * 512

MANUAL = True
TIN_EXIT = (("s", "s"), ("s", "s"))
TOUT_EXIT = (("v", "v"), ("v", "v"))


def tile_mom_kernel(tc, x1, x2, x3, W, b, gamma, beta, running_mean, running_var, out):
    nc = tc.nc
    xs = (x1, x2, x3)
    with ExitStack() as ctx:
        keep = ctx.enter_context(tc.tile_pool(name="keep", bufs=1))
        grp = ctx.enter_context(tc.tile_pool(name="grp", bufs=2))
        code = ctx.enter_context(tc.tile_pool(name="code", bufs=3))
        zpool = ctx.enter_context(tc.tile_pool(name="zpool", bufs=3))
        fpool = ctx.enter_context(tc.tile_pool(name="fpool", bufs=7))
        psum = ctx.enter_context(tc.psum_pool(name="psum", bufs=1))
        if MANUAL:
            ctx.enter_context(tc.manual_schedule())

        counter = [0]

        def bank():
            n = counter[0]
            counter[0] = n + 1
            return psum.tile([P, 512], F32, name="bk%d" % n, tag="bank%d" % (n % 8))

        def copy_out(which, dst, src):
            if which == "s":
                nc.scalar.copy(out=dst, in_=src)
            else:
                nc.vector.tensor_copy(out=dst, in_=src)

        raw = keep.tile([P, 3 * P], BF16, name="raw")
        vraw = keep.tile([P, 3 * P], BF16, name="vraw")

        def load_rows(dst, r0, prm):
            nc.sync.dma_start(
                out=dst[r0:r0 + 16, :],
                in_=prm.rearrange("h e f -> (h e f)").rearrange("(q c) -> q c", q=16),
            )

        load_rows(vraw, 0, running_var)
        one = keep.tile([P, 1], F32, name="one")
        nc.vector.memset(one[:], 1.0)
        raw32 = keep.tile([P, 3 * P], F32, name="raw32")
        nc.vector.memset(raw32[:], 0.0)
        nc.vector.tensor_scalar(
            out=raw32[0:16, :], in0=vraw[0:16, :],
            scalar1=EPS, scalar2=1.0, op0=ALU.add, op1=ALU.mult,
        )
        ident = keep.tile([P, P], F32, name="ident")
        make_identity(nc, ident[:])

        x_sb = {}
        w_sb = [keep.tile([P, HEADS * 4 * D], BF16, name="w_sb%d" % e) for e in range(EXPERTS)]

        def load_w(e, h0, h1):
            nc.sync.dma_start(
                out=w_sb[e][:].rearrange("p (h c) -> p h c", h=HEADS)[:, h0:h1, :],
                in_=W[h0:h1, e].rearrange("h (p t) d -> p h (t d)", t=4),
            )

        def load_x(e, h0, h1):
            xt = keep.tile([P, 4 * D * (h1 - h0)], BF16, name="x_sb%d_%d" % (e, h0))
            nc.sync.dma_start(
                out=xt[:].rearrange("p (j c) -> p j c", j=4),
                in_=xs[e].rearrange("(p j) c -> p j c", j=4)[:, :, D * h0:D * h1],
            )
            for h in range(h0, h1):
                x_sb[(e, h)] = (xt, h - h0, h1 - h0)

        for a in range(2):
            nc.sync.dma_start(
                out=w_sb[0][:, 2 * D * a:2 * D * a + 2 * D],
                in_=W[0, 0].rearrange("(p t) d -> p (t d)", t=4)[:, 2 * D * a:2 * D * a + 2 * D],
            )
        x00 = keep.tile([P, 4 * D], BF16, name="x_sb0_0")
        x_sb[(0, 0)] = (x00, 0, 1)
        nc.sync.dma_start(
            out=x00[:, 0:2 * D].rearrange("p (j c) -> p j c", j=2),
            in_=xs[0].rearrange("(p j) c -> p j c", j=4)[:, 0:2, 0:D],
        )
        for i, prm in enumerate((b, gamma, beta, running_mean)):
            load_rows(raw, 64 + 16 * i, prm)
        nc.sync.dma_start(
            out=x00[:, 2 * D:4 * D].rearrange("p (j c) -> p j c", j=2),
            in_=xs[0].rearrange("(p j) c -> p j c", j=4)[:, 2:4, 0:D],
        )
        junk = keep.tile([P, 1], F32, name="junk")
        nc.scalar.sqrt(out=junk[:], in_=one[:])
        load_w(0, 1, 2)
        load_x(0, 1, 2)
        load_w(0, 2, 3)
        load_x(0, 2, 4)
        load_w(0, 3, 4)
        for e in (1, 2):
            load_x(e, 0, 4)
            load_w(e, 0, 1)
            load_w(e, 1, 2)
            load_w(e, 2, 4)

        nc.scalar.sqrt(out=raw32[0:16, :], in_=raw32[0:16, :])
        nc.scalar.activation(out=junk[:], in_=one[:], func=ACTF.Gelu_apprx_sigmoid)
        nc.gpsimd.tensor_scalar(
            out=raw32[64:128, :], in0=raw[64:128, :],
            scalar1=1.0, scalar2=0.0, op0=ALU.mult, op1=ALU.add,
        )

        NV = 4 * PAIRS
        prm_t = keep.tile([P, P * 3], F32, name="prm_t")
        std_t = prm_t[:, 0:NV]
        bias_t = prm_t[:, 192:192 + NV]
        gamma_t = prm_t[:, 192 + NV:192 + 2 * NV]
        beta_t = prm_t[:, 192 + 2 * NV:192 + 3 * NV]
        mean_t = prm_t[:, 192 + 3 * NV:192 + 4 * NV]
        gain = keep.tile([P, NV], F32, name="gain")
        shift = keep.tile([P, NV], F32, name="shift")

        pbanks = []

        def params_turn():
            pbanks.append(bank())
            for v in range(3):
                nc.tensor.transpose(pbanks[0][:, P * v:P * v + P], raw32[:, P * v:P * v + P], ident[:])

        def params():
            pbank = pbanks[0]
            nc.vector.tensor_copy(
                out=prm_t[:].rearrange("p (r v) -> p r v", v=3),
                in_=pbank[:, 0:3 * P].rearrange("p (v r) -> p r v", v=3),
            )
            nc.vector.reciprocal(out=gain[:], in_=std_t)
            nc.vector.tensor_mul(out=gain[:], in0=gain[:], in1=gamma_t)
            nc.vector.tensor_mul(out=shift[:], in0=mean_t, in1=gain[:])
            nc.vector.tensor_sub(out=shift[:], in0=beta_t, in1=shift[:])

        out_v = out.rearrange("(p j) c -> p j c", j=4)

        codes = {}
        zs = {}

        gtiles = {}
        fins = {}

        def tin_half(k, s, exits):
            e, h = divmod(k, HEADS)
            if s == 0:
                src = w_sb[e][:].bitcast(F32)[:, 1024 * h:1024 * h + 1024]
                g = grp.tile([P, 4 * D], BF16, name="gw", align_bytes=64)
            else:
                xt, hx, nx = x_sb[(e, h)]
                src = xt[:].bitcast(F32)
                g = grp.tile([P, 4 * D], BF16, name="gx", align_bytes=64)
            g32 = g[:].bitcast(F32)
            for a in range(2):
                bk = bank()
                for r in (2 * a, 2 * a + 1):
                    for u in range(2):
                        if s == 0:
                            c0 = 256 * r + P * u
                        else:
                            c0 = 256 * nx * r + 256 * hx + P * u
                        nc.tensor.transpose(
                            bk[:, 256 * u + P * (r - 2 * a):256 * u + P * (r - 2 * a) + P],
                            src[:, c0:c0 + P],
                            ident[:],
                        )
                if s == 0:
                    copy_out(
                        exits[a],
                        g32.rearrange("q (c r u) -> q c r u", r=4, u=2)[:, :, 2 * a:2 * a + 2, :],
                        bk[:].rearrange("q (u r c) -> q c r u", u=2, r=2),
                    )
                else:
                    copy_out(
                        exits[a],
                        g32.rearrange("q (c u) -> q c u", u=2)[:, 256 * a:256 * a + 256, :],
                        bk[:].rearrange("q (u c) -> q c u", u=2),
                    )
            gtiles[(k, s)] = g

        def quant_half(k, s):
            if s == 0:
                c = code.tile([P, D], U32, name="cw", align_bytes=64)
                sc = code.tile([P, D], U8, name="sw", align_bytes=64)
            else:
                c = code.tile([P, D], U32, name="cx", align_bytes=64)
                sc = code.tile([P, D], U8, name="sx", align_bytes=64)
            nc.vector.quantize_mx(out=c[:].bitcast(FP8X4), scales=sc[:], in_=gtiles[(k, s)][:])
            codes[(k, s)] = (c, sc)

        def mx_gelu(k, ts):
            e, h = divmod(k, HEADS)
            cw, sw = codes[(k, 0)]
            cx, sx = codes[(k, 1)]
            accs = {}
            for t in ts:
                acc = bank()
                nc.tensor.matmul_mx(
                    out=acc[:],
                    lhsT=cw[:, P * t:P * t + P].bitcast(FP8X4),
                    lhsT_scale=sw[:, P * t:P * t + P],
                    rhs=cx[:].bitcast(FP8X4),
                    rhs_scale=sx[:],
                    start=True,
                    stop=True,
                )
                accs[t] = acc
            for t in ts:
                col = 4 * (h * EXPERTS + e) + t
                z = zpool.tile([P, 512], F32, name="z%d" % t)
                nc.scalar.activation(
                    out=z[:], in_=accs[t][:], func=ACTF.Gelu_apprx_sigmoid,
                    bias=bias_t[:, col:col + 1], scale=1.0,
                )
                zs[(k, t)] = z

        def affine(k, t):
            e, h = divmod(k, HEADS)
            col = 4 * (h * EXPERTS + e) + t
            z = zs[(k, t)]
            nc.vector.tensor_scalar(
                out=z[:], in0=z[:],
                scalar1=gain[:, col:col + 1], scalar2=shift[:, col:col + 1],
                op0=ALU.mult, op1=ALU.add,
            )

        def fin_copy(k, j, bk, which):
            copy_out(which, fins[k][:, j, :], bk[:])

        def tout_half(k, hf, exits):
            if hf == 0:
                fins[k] = fpool.tile([P, 4, 512], F32, name="fin")
            for j in (2 * hf, 2 * hf + 1):
                bk = bank()
                for t in range(4):
                    nc.tensor.transpose(bk[:, P * t:P * t + P], zs[(k, t)][:, P * j:P * j + P], ident[:])
                fin_copy(k, j, bk, exits[j - 2 * hf])
            nc.sync.dma_start(
                out=out_v[:, 2 * hf:2 * hf + 2, 512 * k:512 * k + 512],
                in_=fins[k][:, 2 * hf:2 * hf + 2, :],
            )

        def tout_last(k):
            fins[k] = fpool.tile([P, 4, 512], F32, name="fin")
            bks = [bank() for j in range(4)]
            for t in range(4):
                for j in range(4):
                    nc.tensor.transpose(bks[j][:, P * t:P * t + P], zs[(k, t)][:, P * j:P * j + P], ident[:])
            for j in range(4):
                fin_copy(k, j, bks[j], ("v", "s")[j % 2])
                nc.sync.dma_start(out=out_v[:, j, 512 * k:512 * k + 512], in_=fins[k][:, j, :])

        tin_half(0, 0, ("v", "v"))
        quant_half(0, 0)
        tin_half(0, 1, ("s", "v"))
        params_turn()
        quant_half(0, 1)
        params()
        pend_q = []
        pend_a = []
        for k in range(0, PAIRS + 1):
            for hf in range(2):
                for kk, s in pend_q:
                    quant_half(kk, s)
                pend_q = []
                if 0 <= k - 2:
                    tout_half(k - 2, hf, ("v", "s") if k - 2 == PAIRS - 2 else TOUT_EXIT[hf])
                for kk, t in pend_a:
                    affine(kk, t)
                pend_a = []
                if k + 1 < PAIRS:
                    tin_half(k + 1, hf, TIN_EXIT[hf])
                    pend_q = [(k + 1, hf)]
                if k < PAIRS:
                    mx_gelu(k, (2 * hf, 2 * hf + 1))
                    pend_a = [(k, 2 * hf), (k, 2 * hf + 1)]
        tout_last(PAIRS - 1)
